import numpy as np
import ml_dtypes


def mxq(x, axis, fmt="e4m3"):
    dtype, down = {"e4m3": (ml_dtypes.float8_e4m3fn, 7), "e5m2": (ml_dtypes.float8_e5m2, 14)}[fmt]
    v = np.moveaxis(np.asarray(x, np.float32).astype(ml_dtypes.bfloat16).astype(np.float64), axis, -1)
    blocks = v.reshape(v.shape[:-1] + (-1, 32))
    amax = np.abs(blocks).max(-1, keepdims=True)
    byte = np.maximum(np.where(amax > 0, np.frexp(amax)[1] - 1 + 127, 0) - down, 1)
    scale = np.exp2(byte - 127.0)
    codes = (blocks / scale).astype(np.float32).astype(dtype).astype(np.float64)
    return np.moveaxis((codes * scale).reshape(v.shape), -1, axis)


WIDE = False


def mx_kscale(k):
    if not WIDE:
        return np.ones(k)
    levels = np.array([10, -10, 5, -5, 0])
    a = np.random.permutation(np.resize(levels, k // 512 * 4)).reshape(k // 512, 4)
    idx = np.arange(k)
    return np.exp2(a[idx // 512, idx % 128 // 32])


BF16 = ml_dtypes.bfloat16


def bf(x):
    return np.asarray(x, np.float32).astype(BF16)


def f64(x):
    return np.asarray(x).astype(np.float64)


E2M1 = np.array([0.0, 0.5, 1.0, 1.5, 2.0, 3.0, 4.0, 6.0, -0.0, -0.5, -1.0, -1.5, -2.0, -3.0, -4.0, -6.0])


def pack_weight(w, fmt):
    k, n = w.shape
    w = f64(bf(w)).reshape(k // 32, 32, n)
    amax = np.abs(w).max(1)
    if fmt == "e4m3":
        byte = np.frexp(amax)[1] - 1 + 127 - 7
    else:
        mant, ex = np.frexp(amax / 6.0)
        byte = np.where(mant > 0.5, ex, ex - 1) + 127
    byte = np.clip(np.where(amax > 0, byte, 1), 1, 254)
    scaled = (w * np.exp2(127.0 - byte)[:, None, :]).reshape(k, n).astype(np.float32)
    by_word = np.ascontiguousarray(scaled.reshape(k // 512, 128, 4, n).transpose(0, 1, 3, 2))
    if fmt == "e4m3":
        words = by_word.astype(ml_dtypes.float8_e4m3fn).view(np.uint8)
    else:
        c = by_word.astype(ml_dtypes.float4_e2m1fn).view(np.uint8) & 0xF
        words = c[..., 0::2] | (c[..., 1::2] << 4)
    return np.ascontiguousarray(words), np.ascontiguousarray(byte.astype(np.uint8).reshape(k // 512, 16, n))


def unpack_weight(words, scales, fmt):
    g, p, n, _ = words.shape
    if fmt == "e4m3":
        vals = np.ascontiguousarray(words).view(ml_dtypes.float8_e4m3fn).astype(np.float64)
    else:
        nib = np.empty((g, p, n, 4), np.uint8)
        nib[..., 0::2] = words & 0xF
        nib[..., 1::2] = words >> 4
        vals = E2M1[nib]
    vals = vals * np.repeat(np.exp2(scales.astype(np.float64) - 127.0), 8, axis=1)[..., None]
    return vals.transpose(0, 1, 3, 2).reshape(g * 512, n)


B, X, N, OS = 128, 2048, 6144, 2048
H = N - OS


def setup_inputs():
    s, t = mx_kscale(X), mx_kscale(H)
    std0 = np.sqrt(2.0 / X)
    std1 = np.sqrt(2.0 / (X + H))
    row_scale = np.concatenate([std0 * t, np.full(OS, std1)])
    bias_scale = np.concatenate([t, np.ones(OS)])
    x = bf(np.random.standard_normal((B, X)) * s)
    w0_words, w0_scales = pack_weight((np.random.standard_normal((N, X)) * row_scale[:, None] / s).T, "e4m3")
    w1_words, w1_scales = pack_weight((np.random.standard_normal((OS, H)) * std1 / t).T, "e4m3")
    biases = bf(np.random.random(N) * bias_scale)
    return {"x": x,
            "w0_words": w0_words, "w0_scales": w0_scales,
            "w1_words": w1_words, "w1_scales": w1_scales,
            "biases": biases}


def reference(x, w0_words, w0_scales, w1_words, w1_scales, biases):
    n = w0_words.shape[2]
    os_ = w1_words.shape[2]
    z = (mxq(f64(x), 1, "e4m3") @ unpack_weight(w0_words, w0_scales, "e4m3")) + f64(biases)
    h = np.maximum(z[:, : n - os_], 0.0)
    return z[:, n - os_:] + (mxq(h, 1, "e4m3") @ unpack_weight(w1_words, w1_scales, "e4m3"))

@@ -1,0 +1,184 @@
+import concourse.bass as bass
+import concourse.mybir as mybir
+import concourse.tile as tile
+from concourse.masks import make_identity
+
+F32 = mybir.dt.float32
+BF16 = mybir.dt.bfloat16
+I32 = mybir.dt.int32
+U32 = mybir.dt.uint32
+U8 = mybir.dt.uint8
+FP8X4 = mybir.dt.float8_e4m3fn_x4
+ADD = mybir.AluOpType.add
+RELU = mybir.ActivationFunctionType.Relu
+
+P = 128
+B = 128
+X = 2048
+H = 4096
+OS = 2048
+NT = 512
+GX = X // 512
+GH = H // 512
+CO = OS // NT
+
+FLOPS = 2 * B * X * (H + OS) + 2 * B * H * OS
+
+
+def tile_spn_w_kernel(tc, x, w0_words, w0_scales, w1_words, w1_scales, biases, out):
+    nc = tc.nc
+    with tc.tile_pool(name="keep", bufs=1) as keep, tc.psum_pool(name="psum", bufs=1) as psum, tc.manual_schedule():
+        x_sb = keep.tile([P, X], BF16, name="x_sb")
+        pl0 = keep.tile([P, H + OS], U8, name="pl0", align_bytes=64)
+        pl1 = [keep.tile([P, OS], U8, name="pl1_%d" % a, align_bytes=64) for a in range(2)]
+        bt = keep.tile([P, P], BF16, name="bt")
+        ident_b = keep.tile([P, P], BF16, name="ident_b")
+        ident_f = keep.tile([P, P], F32, name="ident_f")
+        w0h = [keep.tile([P, H], U32, name="w0h_%d" % g, align_bytes=64) for g in range(GX)]
+        w0o = [keep.tile([P, OS], U32, name="w0o_%d" % g, align_bytes=64) for g in range(GX)]
+        w1 = [keep.tile([P, OS], U32, name="w1_%d" % g, align_bytes=64) for g in range(GH - 1)]
+        w1l = [keep.tile([P, NT], U32, name="w1l_%d" % c, align_bytes=64) for c in range(CO)]
+
+        nc.sync.dma_start(out=x_sb[:], in_=x)
+        nc.vector.memset(bt[:], 0.0)
+        nc.vector.memset(pl0[:].bitcast(I32), 0)
+        for a in range(2):
+            nc.vector.memset(pl1[a][:].bitcast(I32), 0)
+        make_identity(nc, ident_f[:])
+        make_identity(nc, ident_b[:])
+        nc.scalar.dma_start(out=bt[0:48, :], in_=biases.rearrange("(c n) -> c n", n=P))
+        for q in range(4):
+            nc.sync.dma_start(
+                out=pl0[32 * q : 32 * q + 16, :].bitcast(I32),
+                in_=w0_scales[:, 4 * q : 4 * q + 4, :].bitcast(I32),
+            )
+        for a in range(2):
+            for q in range(4):
+                nc.sync.dma_start(
+                    out=pl1[a][32 * q : 32 * q + 16, :].bitcast(I32),
+                    in_=w1_scales[4 * a : 4 * a + 4, 4 * q : 4 * q + 4, :].bitcast(I32),
+                )
+        for g in range(GX):
+            nc.sync.dma_start(
+                out=w0h[g][:].bitcast(I32),
+                in_=w0_words[g].rearrange("p n t -> p (n t)")[:, 0 : 4 * H].bitcast(I32),
+            )
+        for g in range(GX):
+            nc.sync.dma_start(
+                out=w0o[g][:].bitcast(I32),
+                in_=w0_words[g].rearrange("p n t -> p (n t)")[:, 4 * H : 4 * (H + OS)].bitcast(I32),
+            )
+        for g in range(GH - 1):
+            nc.sync.dma_start(
+                out=w1[g][:].bitcast(I32),
+                in_=w1_words[g].rearrange("p n t -> p (n t)").bitcast(I32),
+            )
+        for c in range(CO):
+            nc.sync.dma_start(
+                out=w1l[c][:].bitcast(I32),
+                in_=w1_words[GH - 1].rearrange("p n t -> p (n t)")[:, 4 * NT * c : 4 * NT * (c + 1)].bitcast(I32),
+            )
+
+        xg = keep.tile([P, GX * B * 4], BF16, name="xg", align_bytes=64)
+        xq = keep.tile([P, GX * B], U32, name="xq", align_bytes=64)
+        xs = keep.tile([P, GX * B], U8, name="xs", align_bytes=64)
+        x32 = x_sb[:].bitcast(F32)
+        xg32 = xg[:].bitcast(F32).rearrange("p (g b u) -> p g b u", g=GX, u=2)
+        for hf in range(2):
+            xt = psum.tile([P, 2, 2, B], F32, name="xt_%d" % hf, tag="b%d" % hf)
+            for gl in range(2):
+                g = 2 * hf + gl
+                for u in range(2):
+                    nc.tensor.transpose(xt[:, gl, u, :], x32[:, 256 * g + u : 256 * (g + 1) : 2], ident_f[:])
+            src = xt[:].rearrange("p g u b -> p g b u")
+            if hf == 0:
+                nc.vector.tensor_copy(out=xg32[:, 0:2], in_=src)
+            else:
+                nc.scalar.copy(out=xg32[:, 2:4], in_=src)
+        nc.vector.quantize_mx(out=xq[:].bitcast(FP8X4), scales=xs[:], in_=xg[:])
+
+        bias_h = [keep.tile([P, 4, P], BF16, name="bias_h_%d" % j) for j in range(GH)]
+        bias_o = [keep.tile([P, NT], BF16, name="bias_o_%d" % c) for c in range(CO)]
+        for i in range(GH + CO):
+            pb = psum.tile([P, NT], F32, name="pb_%d" % i, tag="b%d" % (2 + i % 6))
+            for s in range(4):
+                c = 4 * i + s
+                nc.tensor.matmul(
+                    out=pb[:, P * s : P * (s + 1)],
+                    lhsT=ident_b[:, c : c + 1].to_broadcast([P, P]),
+                    rhs=bt[:],
+                    start=True,
+                    stop=True,
+                )
+            if i < GH:
+                dst = bias_h[i][:]
+                src = pb[:].rearrange("b (p t) -> b t p", t=4)
+            else:
+                dst = bias_o[i - GH][:]
+                src = pb[:]
+            if i % 2 == 0:
+                nc.vector.tensor_copy(out=dst, in_=src)
+            else:
+                nc.scalar.copy(out=dst, in_=src)
+
+        def x_pass(acc, g, words, col0, start, stop):
+            nc.tensor.matmul_mx(
+                out=acc,
+                lhsT=xq[:, B * g : B * (g + 1)].bitcast(FP8X4),
+                lhsT_scale=xs[:, B * g : B * (g + 1)],
+                rhs=words.bitcast(FP8X4),
+                rhs_scale=pl0[4 * g : P, col0 : col0 + NT],
+                start=start,
+                stop=stop,
+            )
+
+        ph = [psum.tile([P, NT], F32, name="ph_%d" % j, tag="b%d" % j) for j in range(GH)]
+        for g in range(GX):
+            for j in range(GH):
+                x_pass(ph[j][:], g, w0h[g][:, NT * j : NT * (j + 1)], NT * j, g == 0, g == GX - 1)
+
+        zb = [keep.tile([P, 4, P], BF16, name="zb_%d" % j) for j in range(GH)]
+        hg = [keep.tile([P, 2, B, 4], BF16, name="hg_%d" % jj, align_bytes=64) for jj in range(GH // 2)]
+        hq = [keep.tile([P, 2 * B], U32, name="hq_%d" % jj, align_bytes=64) for jj in range(GH // 2)]
+        hs = [keep.tile([P, 2 * B], U8, name="hs_%d" % jj, align_bytes=64) for jj in range(GH // 2)]
+        for jj in range(GH // 2):
+            for jl in range(2):
+                j = 2 * jj + jl
+                nc.vector.tensor_tensor(
+                    out=zb[j][:],
+                    in0=ph[j][:].rearrange("b (p t) -> b t p", t=4),
+                    in1=bias_h[j][:],
+                    op=ADD,
+                )
+            tp = psum.tile([P, 2, 4, B], BF16, name="tp_%d" % jj, tag="b%d" % jj)
+            for jl in range(2):
+                for t in range(4):
+                    nc.tensor.transpose(tp[:, jl, t, :], zb[2 * jj + jl][:, t, :], ident_b[:])
+            nc.scalar.activation(out=hg[jj][:], in_=tp[:].rearrange("p j t b -> p j b t"), func=RELU)
+        for jj in range(GH // 2):
+            nc.vector.quantize_mx(
+                out=hq[jj][:].bitcast(FP8X4),
+                scales=hs[jj][:],
+                in_=hg[jj][:].rearrange("p j b t -> p (j b t)"),
+            )
+
+        po = [psum.tile([P, NT], F32, name="po_%d" % c, tag="b%d" % (4 + c)) for c in range(CO)]
+        for g in range(GX):
+            for c in range(CO):
+                x_pass(po[c][:], g, w0o[g][:, NT * c : NT * (c + 1)], H + NT * c, g == 0, False)
+        for g in range(GH):
+            for c in range(CO):
+                words = w1[g][:, NT * c : NT * (c + 1)] if g < GH - 1 else w1l[c][:]
+                nc.tensor.matmul_mx(
+                    out=po[c][:],
+                    lhsT=hq[g // 2][:, B * (g % 2) : B * (g % 2 + 1)].bitcast(FP8X4),
+                    lhsT_scale=hs[g // 2][:, B * (g % 2) : B * (g % 2 + 1)],
+                    rhs=words.bitcast(FP8X4),
+                    rhs_scale=pl1[g // 4][4 * (g % 4) : P, NT * c : NT * (c + 1)],
+                    start=False,
+                    stop=(g == GH - 1),
+                )
+        for c in range(CO):
+            o_sb = keep.tile([P, NT], F32, name="o_sb_%d" % c)
+            nc.vector.tensor_tensor(out=o_sb[:], in0=po[c][:], in1=bias_o[c][:], op=ADD)
+            nc.sync.dma_start(out=out[:, NT * c : NT * (c + 1)], in_=o_sb[:])

@@ -21,6 +21,8 @@ NT = 512
 GX = X // 512
 GH = H // 512
 CO = OS // NT
+CA = 3
+LAST = ((0, 5), (5, 2), (7, 1))
 
 FLOPS = 2 * B * X * (H + OS) + 2 * B * H * OS
 
@@ -36,8 +38,8 @@ def tile_spn_w_kernel(tc, x, w0_words, w0_scales, w1_words, w1_scales, biases, o
         ident_f = keep.tile([P, P], F32, name="ident_f")
         w0h = [keep.tile([P, H], U32, name="w0h_%d" % g, align_bytes=64) for g in range(GX)]
         w0o = [keep.tile([P, OS], U32, name="w0o_%d" % g, align_bytes=64) for g in range(GX)]
-        w1 = [keep.tile([P, OS], U32, name="w1_%d" % g, align_bytes=64) for g in range(GH - 1)]
-        w1l = [keep.tile([P, NT], U32, name="w1l_%d" % c, align_bytes=64) for c in range(CO)]
+        w1a = [keep.tile([P, 2, CA * NT], U32, name="w1a_%d" % i, align_bytes=64) for i in range(GH // 2)]
+        w1b = [keep.tile([P, n, NT], U32, name="w1b_%d" % i, align_bytes=64) for i, (g0, n) in enumerate(LAST)]
 
         nc.sync.dma_start(out=x_sb[:], in_=x)
         nc.vector.memset(bt[:], 0.0)
@@ -68,15 +70,15 @@ def tile_spn_w_kernel(tc, x, w0_words, w0_scales, w1_words, w1_scales, biases, o
                 out=w0o[g][:].bitcast(I32),
                 in_=w0_words[g].rearrange("p n t -> p (n t)")[:, 4 * H : 4 * (H + OS)].bitcast(I32),
             )
-        for g in range(GH - 1):
+        for i in range(GH // 2):
             nc.sync.dma_start(
-                out=w1[g][:].bitcast(I32),
-                in_=w1_words[g].rearrange("p n t -> p (n t)").bitcast(I32),
+                out=w1a[i][:].bitcast(I32),
+                in_=w1_words[2 * i : 2 * i + 2].rearrange("g p n t -> p g (n t)")[:, :, 0 : 4 * NT * CA].bitcast(I32),
             )
-        for c in range(CO):
+        for i, (g0, n) in enumerate(LAST):
             nc.sync.dma_start(
-                out=w1l[c][:].bitcast(I32),
-                in_=w1_words[GH - 1].rearrange("p n t -> p (n t)")[:, 4 * NT * c : 4 * NT * (c + 1)].bitcast(I32),
+                out=w1b[i][:].bitcast(I32),
+                in_=w1_words[g0 : g0 + n].rearrange("g p n t -> p g (n t)")[:, :, 4 * NT * CA : 4 * OS].bitcast(I32),
             )
 
         xg = keep.tile([P, GX * B * 4], BF16, name="xg", align_bytes=64)
@@ -166,19 +168,28 @@ def tile_spn_w_kernel(tc, x, w0_words, w0_scales, w1_words, w1_scales, biases, o
         for g in range(GX):
             for c in range(CO):
                 x_pass(po[c][:], g, w0o[g][:, NT * c : NT * (c + 1)], H + NT * c, g == 0, False)
+
+        def h_pass(c, g, words):
+            nc.tensor.matmul_mx(
+                out=po[c][:],
+                lhsT=hq[g // 2][:, B * (g % 2) : B * (g % 2 + 1)].bitcast(FP8X4),
+                lhsT_scale=hs[g // 2][:, B * (g % 2) : B * (g % 2 + 1)],
+                rhs=words.bitcast(FP8X4),
+                rhs_scale=pl1[g // 4][4 * (g % 4) : P, NT * c : NT * (c + 1)],
+                start=False,
+                stop=(g == GH - 1),
+            )
+
+        o_a = keep.tile([P, CA * NT], F32, name="o_a")
+        o_b = keep.tile([P, NT], F32, name="o_b")
         for g in range(GH):
-            for c in range(CO):
-                words = w1[g][:, NT * c : NT * (c + 1)] if g < GH - 1 else w1l[c][:]
-                nc.tensor.matmul_mx(
-                    out=po[c][:],
-                    lhsT=hq[g // 2][:, B * (g % 2) : B * (g % 2 + 1)].bitcast(FP8X4),
-                    lhsT_scale=hs[g // 2][:, B * (g % 2) : B * (g % 2 + 1)],
-                    rhs=words.bitcast(FP8X4),
-                    rhs_scale=pl1[g // 4][4 * (g % 4) : P, NT * c : NT * (c + 1)],
-                    start=False,
-                    stop=(g == GH - 1),
-                )
-        for c in range(CO):
-            o_sb = keep.tile([P, NT], F32, name="o_sb_%d" % c)
-            nc.vector.tensor_tensor(out=o_sb[:], in0=po[c][:], in1=bias_o[c][:], op=ADD)
-            nc.sync.dma_start(out=out[:, NT * c : NT * (c + 1)], in_=o_sb[:])
+            for c in range(CA):
+                h_pass(c, g, w1a[g // 2][:, g % 2, NT * c : NT * (c + 1)])
+        for c in range(CA):
+            nc.vector.tensor_tensor(out=o_a[:, NT * c : NT * (c + 1)], in0=po[c][:], in1=bias_o[c][:], op=ADD)
+        nc.sync.dma_start(out=out[:, 0 : NT * CA], in_=o_a[:])
+        for i, (g0, n) in enumerate(LAST):
+            for gl in range(n):
+                h_pass(CO - 1, g0 + gl, w1b[i][:, gl, :])
+        nc.vector.tensor_tensor(out=o_b[:], in0=po[CO - 1][:], in1=bias_o[CO - 1][:], op=ADD)
+        nc.sync.dma_start(out=out[:, NT * CA : OS], in_=o_b[:])

@@ -21,8 +21,16 @@ NT = 512
 GX = X // 512
 GH = H // 512
 CO = OS // NT
-CA = 3
-LAST = ((0, 5), (5, 2), (7, 1))
+W1_LOADS = (
+    (0, 2, 0, 4),
+    (2, 2, 0, 4),
+    (4, 2, 0, 3),
+    (6, 1, 0, 3),
+    (7, 1, 0, 3),
+    (4, 2, 3, 1),
+    (6, 1, 3, 1),
+    (7, 1, 3, 1),
+)
 
 FLOPS = 2 * B * X * (H + OS) + 2 * B * H * OS
 
@@ -38,8 +46,9 @@ def tile_spn_w_kernel(tc, x, w0_words, w0_scales, w1_words, w1_scales, biases, o
         ident_f = keep.tile([P, P], F32, name="ident_f")
         w0h = [keep.tile([P, H], U32, name="w0h_%d" % g, align_bytes=64) for g in range(GX)]
         w0o = [keep.tile([P, OS], U32, name="w0o_%d" % g, align_bytes=64) for g in range(GX)]
-        w1a = [keep.tile([P, 2, CA * NT], U32, name="w1a_%d" % i, align_bytes=64) for i in range(GH // 2)]
-        w1b = [keep.tile([P, n, NT], U32, name="w1b_%d" % i, align_bytes=64) for i, (g0, n) in enumerate(LAST)]
+        w1 = [
+            keep.tile([P, n, w * NT], U32, name="w1_%d" % i, align_bytes=64) for i, (g0, n, c0, w) in enumerate(W1_LOADS)
+        ]
 
         nc.sync.dma_start(out=x_sb[:], in_=x)
         nc.vector.memset(bt[:], 0.0)
@@ -70,15 +79,12 @@ def tile_spn_w_kernel(tc, x, w0_words, w0_scales, w1_words, w1_scales, biases, o
                 out=w0o[g][:].bitcast(I32),
                 in_=w0_words[g].rearrange("p n t -> p (n t)")[:, 4 * H : 4 * (H + OS)].bitcast(I32),
             )
-        for i in range(GH // 2):
+        for i, (g0, n, c0, w) in enumerate(W1_LOADS):
             nc.sync.dma_start(
-                out=w1a[i][:].bitcast(I32),
-                in_=w1_words[2 * i : 2 * i + 2].rearrange("g p n t -> p g (n t)")[:, :, 0 : 4 * NT * CA].bitcast(I32),
-            )
-        for i, (g0, n) in enumerate(LAST):
-            nc.sync.dma_start(
-                out=w1b[i][:].bitcast(I32),
-                in_=w1_words[g0 : g0 + n].rearrange("g p n t -> p g (n t)")[:, :, 4 * NT * CA : 4 * OS].bitcast(I32),
+                out=w1[i][:].bitcast(I32),
+                in_=w1_words[g0 : g0 + n].rearrange("g p n t -> p g (n t)")[
+                    :, :, 4 * NT * c0 : 4 * NT * (c0 + w)
+                ].bitcast(I32),
             )
 
         xg = keep.tile([P, GX * B * 4], BF16, name="xg", align_bytes=64)
@@ -180,16 +186,15 @@ def tile_spn_w_kernel(tc, x, w0_words, w0_scales, w1_words, w1_scales, biases, o
                 stop=(g == GH - 1),
             )
 
-        o_a = keep.tile([P, CA * NT], F32, name="o_a")
-        o_b = keep.tile([P, NT], F32, name="o_b")
-        for g in range(GH):
-            for c in range(CA):
-                h_pass(c, g, w1a[g // 2][:, g % 2, NT * c : NT * (c + 1)])
-        for c in range(CA):
-            nc.vector.tensor_tensor(out=o_a[:, NT * c : NT * (c + 1)], in0=po[c][:], in1=bias_o[c][:], op=ADD)
-        nc.sync.dma_start(out=out[:, 0 : NT * CA], in_=o_a[:])
-        for i, (g0, n) in enumerate(LAST):
+        for i, (g0, n, c0, w) in enumerate(W1_LOADS):
             for gl in range(n):
-                h_pass(CO - 1, g0 + gl, w1b[i][:, gl, :])
-        nc.vector.tensor_tensor(out=o_b[:], in0=po[CO - 1][:], in1=bias_o[CO - 1][:], op=ADD)
-        nc.sync.dma_start(out=out[:, NT * CA : OS], in_=o_b[:])
+                for c in range(w):
+                    h_pass(c0 + c, g0 + gl, w1[i][:, gl, NT * c : NT * (c + 1)])
+            if g0 + n < GH:
+                continue
+            o_sb = keep.tile([P, w * NT], F32, name="o_sb_%d" % c0)
+            for c in range(w):
+                nc.vector.tensor_tensor(
+                    out=o_sb[:, NT * c : NT * (c + 1)], in0=po[c0 + c][:], in1=bias_o[c0 + c][:], op=ADD
+                )
+            nc.sync.dma_start(out=out[:, NT * c0 : NT * (c0 + w)], in_=o_sb[:])

@@ -58,17 +58,18 @@ def tile_spn_w_kernel(tc, x, w0_words, w0_scales, w1_words, w1_scales, biases, o
         make_identity(nc, ident_f[:])
         make_identity(nc, ident_b[:])
         nc.scalar.dma_start(out=bt[0:48, :], in_=biases.rearrange("(c n) -> c n", n=P))
-        for q in range(4):
-            nc.sync.dma_start(
-                out=pl0[32 * q : 32 * q + 16, :].bitcast(I32),
-                in_=w0_scales[:, 4 * q : 4 * q + 4, :].bitcast(I32),
-            )
-        for a in range(2):
-            for q in range(4):
+        for qs in ((2, 3), (0, 1)):
+            for q in qs:
                 nc.sync.dma_start(
-                    out=pl1[a][32 * q : 32 * q + 16, :].bitcast(I32),
-                    in_=w1_scales[4 * a : 4 * a + 4, 4 * q : 4 * q + 4, :].bitcast(I32),
+                    out=pl0[32 * q : 32 * q + 16, :].bitcast(I32),
+                    in_=w0_scales[:, 4 * q : 4 * q + 4, :].bitcast(I32),
                 )
+            for a in range(2):
+                for q in qs:
+                    nc.sync.dma_start(
+                        out=pl1[a][32 * q : 32 * q + 16, :].bitcast(I32),
+                        in_=w1_scales[4 * a : 4 * a + 4, 4 * q : 4 * q + 4, :].bitcast(I32),
+                    )
         for g in range(GX):
             nc.sync.dma_start(
                 out=w0h[g][:].bitcast(I32),

@@ -193,9 +193,11 @@ def tile_spn_w_kernel(tc, x, w0_words, w0_scales, w1_words, w1_scales, biases, o
                     h_pass(c0 + c, g0 + gl, w1[i][:, gl, NT * c : NT * (c + 1)])
             if g0 + n < GH:
                 continue
-            o_sb = keep.tile([P, w * NT], F32, name="o_sb_%d" % c0)
-            for c in range(w):
+            wo = NT if c0 + w < CO else NT // 2
+            for lo in range(NT * c0, NT * (c0 + w), wo):
+                c, off = divmod(lo, NT)
+                o_sb = keep.tile([P, wo], F32, name="o_sb_%d" % lo)
                 nc.vector.tensor_tensor(
-                    out=o_sb[:, NT * c : NT * (c + 1)], in0=po[c0 + c][:], in1=bias_o[c0 + c][:], op=ADD
+                    out=o_sb[:], in0=po[c][:, off : off + wo], in1=bias_o[c][:, off : off + wo], op=ADD
                 )
-            nc.sync.dma_start(out=out[:, NT * c0 : NT * (c0 + w)], in_=o_sb[:])
+                nc.sync.dma_start(out=out[:, lo : lo + wo], in_=o_sb[:])

@@ -44,8 +44,9 @@ def tile_spn_w_kernel(tc, x, w0_words, w0_scales, w1_words, w1_scales, biases, o
         bt = keep.tile([P, P], BF16, name="bt")
         ident_b = keep.tile([P, P], BF16, name="ident_b")
         ident_f = keep.tile([P, P], F32, name="ident_f")
-        w0h = [keep.tile([P, H], U32, name="w0h_%d" % g, align_bytes=64) for g in range(GX)]
-        w0o = [keep.tile([P, OS], U32, name="w0o_%d" % g, align_bytes=64) for g in range(GX)]
+        w0 = [keep.tile([P, H + OS], U32, name="w0_%d" % g, align_bytes=64) for g in range(GX - 1)]
+        w0h = keep.tile([P, H], U32, name="w0h", align_bytes=64)
+        w0o = keep.tile([P, OS], U32, name="w0o", align_bytes=64)
         w1 = [
             keep.tile([P, n, w * NT], U32, name="w1_%d" % i, align_bytes=64) for i, (g0, n, c0, w) in enumerate(W1_LOADS)
         ]
@@ -70,16 +71,11 @@ def tile_spn_w_kernel(tc, x, w0_words, w0_scales, w1_words, w1_scales, biases, o
                         out=pl1[a][32 * q : 32 * q + 16, :].bitcast(I32),
                         in_=w1_scales[4 * a : 4 * a + 4, 4 * q : 4 * q + 4, :].bitcast(I32),
                     )
-        for g in range(GX):
-            nc.sync.dma_start(
-                out=w0h[g][:].bitcast(I32),
-                in_=w0_words[g].rearrange("p n t -> p (n t)")[:, 0 : 4 * H].bitcast(I32),
-            )
-        for g in range(GX):
-            nc.sync.dma_start(
-                out=w0o[g][:].bitcast(I32),
-                in_=w0_words[g].rearrange("p n t -> p (n t)")[:, 4 * H : 4 * (H + OS)].bitcast(I32),
-            )
+        for g in range(GX - 1):
+            nc.sync.dma_start(out=w0[g][:].bitcast(I32), in_=w0_words[g].rearrange("p n t -> p (n t)").bitcast(I32))
+        last = w0_words[GX - 1].rearrange("p n t -> p (n t)")
+        nc.sync.dma_start(out=w0h[:].bitcast(I32), in_=last[:, 0 : 4 * H].bitcast(I32))
+        nc.sync.dma_start(out=w0o[:].bitcast(I32), in_=last[:, 4 * H : 4 * (H + OS)].bitcast(I32))
         for i, (g0, n, c0, w) in enumerate(W1_LOADS):
             nc.sync.dma_start(
                 out=w1[i][:].bitcast(I32),
@@ -144,7 +140,8 @@ def tile_spn_w_kernel(tc, x, w0_words, w0_scales, w1_words, w1_scales, biases, o
         ph = [psum.tile([P, NT], F32, name="ph_%d" % j, tag="b%d" % j) for j in range(GH)]
         for g in range(GX):
             for j in range(GH):
-                x_pass(ph[j][:], g, w0h[g][:, NT * j : NT * (j + 1)], NT * j, g == 0, g == GX - 1)
+                words = w0[g] if g < GX - 1 else w0h
+                x_pass(ph[j][:], g, words[:, NT * j : NT * (j + 1)], NT * j, g == 0, g == GX - 1)
 
         zb = [keep.tile([P, 4, P], BF16, name="zb_%d" % j) for j in range(GH)]
         hg = [keep.tile([P, 2, B, 4], BF16, name="hg_%d" % jj, align_bytes=64) for jj in range(GH // 2)]
@@ -174,7 +171,8 @@ def tile_spn_w_kernel(tc, x, w0_words, w0_scales, w1_words, w1_scales, biases, o
         po = [psum.tile([P, NT], F32, name="po_%d" % c, tag="b%d" % (4 + c)) for c in range(CO)]
         for g in range(GX):
             for c in range(CO):
-                x_pass(po[c][:], g, w0o[g][:, NT * c : NT * (c + 1)], H + NT * c, g == 0, False)
+                words = w0[g][:, H:] if g < GX - 1 else w0o
+                x_pass(po[c][:], g, words[:, NT * c : NT * (c + 1)], H + NT * c, g == 0, False)
 
         def h_pass(c, g, words):
             nc.tensor.matmul_mx(

@@ -52,25 +52,25 @@ def tile_spn_w_kernel(tc, x, w0_words, w0_scales, w1_words, w1_scales, biases, o
         ]
 
         nc.sync.dma_start(out=x_sb[:], in_=x)
-        nc.vector.memset(bt[:], 0.0)
-        nc.vector.memset(pl0[:].bitcast(I32), 0)
+        nc.gpsimd.memset(bt[:], 0.0)
         for a in range(2):
             nc.vector.memset(pl1[a][:].bitcast(I32), 0)
+        nc.vector.memset(pl0[:].bitcast(I32), 0)
         make_identity(nc, ident_f[:])
         make_identity(nc, ident_b[:])
         nc.scalar.dma_start(out=bt[0:48, :], in_=biases.rearrange("(c n) -> c n", n=P))
         for qs in ((2, 3), (0, 1)):
-            for q in qs:
-                nc.sync.dma_start(
-                    out=pl0[32 * q : 32 * q + 16, :].bitcast(I32),
-                    in_=w0_scales[:, 4 * q : 4 * q + 4, :].bitcast(I32),
-                )
             for a in range(2):
                 for q in qs:
                     nc.sync.dma_start(
                         out=pl1[a][32 * q : 32 * q + 16, :].bitcast(I32),
                         in_=w1_scales[4 * a : 4 * a + 4, 4 * q : 4 * q + 4, :].bitcast(I32),
                     )
+            for q in qs:
+                nc.sync.dma_start(
+                    out=pl0[32 * q : 32 * q + 16, :].bitcast(I32),
+                    in_=w0_scales[:, 4 * q : 4 * q + 4, :].bitcast(I32),
+                )
         for g in range(GX - 1):
             nc.sync.dma_start(out=w0[g][:].bitcast(I32), in_=w0_words[g].rearrange("p n t -> p (n t)").bitcast(I32))
         last = w0_words[GX - 1].rearrange("p n t -> p (n t)")

import concourse.bass as bass
import concourse.mybir as mybir
import concourse.tile as tile
from concourse.masks import make_identity

F32 = mybir.dt.float32
BF16 = mybir.dt.bfloat16
I32 = mybir.dt.int32
U32 = mybir.dt.uint32
U8 = mybir.dt.uint8
FP8X4 = mybir.dt.float8_e4m3fn_x4
ADD = mybir.AluOpType.add
RELU = mybir.ActivationFunctionType.Relu

P = 128
B = 128
X = 2048
H = 4096
OS = 2048
NT = 512
GX = X // 512
GH = H // 512
CO = OS // NT
W1_LOADS = (
    (0, 2, 0, 4),
    (2, 2, 0, 4),
    (4, 2, 0, 3),
    (6, 1, 0, 3),
    (7, 1, 0, 3),
    (4, 2, 3, 1),
    (6, 1, 3, 1),
    (7, 1, 3, 1),
)

FLOPS = 2 * B * X * (H + OS) + 2 * B * H * OS


def tile_spn_w_kernel(tc, x, w0_words, w0_scales, w1_words, w1_scales, biases, out):
    nc = tc.nc
    with tc.tile_pool(name="keep", bufs=1) as keep, tc.psum_pool(name="psum", bufs=1) as psum, tc.manual_schedule():
        x_sb = keep.tile([P, X], BF16, name="x_sb")
        pl0 = keep.tile([P, H + OS], U8, name="pl0", align_bytes=64)
        pl1 = [keep.tile([P, OS], U8, name="pl1_%d" % a, align_bytes=64) for a in range(2)]
        bt = keep.tile([P, P], BF16, name="bt")
        ident_b = keep.tile([P, P], BF16, name="ident_b")
        ident_f = keep.tile([P, P], F32, name="ident_f")
        w0 = [keep.tile([P, H + OS], U32, name="w0_%d" % g, align_bytes=64) for g in range(GX - 1)]
        w0h = keep.tile([P, H], U32, name="w0h", align_bytes=64)
        w0o = keep.tile([P, OS], U32, name="w0o", align_bytes=64)
        w1 = [
            keep.tile([P, n, w * NT], U32, name="w1_%d" % i, align_bytes=64) for i, (g0, n, c0, w) in enumerate(W1_LOADS)
        ]

        nc.sync.dma_start(out=x_sb[:], in_=x)
        nc.gpsimd.memset(bt[:], 0.0)
        for a in range(2):
            nc.vector.memset(pl1[a][:].bitcast(I32), 0)
        nc.vector.memset(pl0[:].bitcast(I32), 0)
        make_identity(nc, ident_f[:])
        make_identity(nc, ident_b[:])
        nc.scalar.dma_start(out=bt[0:48, :], in_=biases.rearrange("(c n) -> c n", n=P))
        for qs in ((2, 3), (0, 1)):
            for a in range(2):
                for q in qs:
                    nc.sync.dma_start(
                        out=pl1[a][32 * q : 32 * q + 16, :].bitcast(I32),
                        in_=w1_scales[4 * a : 4 * a + 4, 4 * q : 4 * q + 4, :].bitcast(I32),
                    )
            for q in qs:
                nc.sync.dma_start(
                    out=pl0[32 * q : 32 * q + 16, :].bitcast(I32),
                    in_=w0_scales[:, 4 * q : 4 * q + 4, :].bitcast(I32),
                )
        for g in range(GX - 1):
            nc.sync.dma_start(out=w0[g][:].bitcast(I32), in_=w0_words[g].rearrange("p n t -> p (n t)").bitcast(I32))
        last = w0_words[GX - 1].rearrange("p n t -> p (n t)")
        nc.sync.dma_start(out=w0h[:].bitcast(I32), in_=last[:, 0 : 4 * H].bitcast(I32))
        nc.sync.dma_start(out=w0o[:].bitcast(I32), in_=last[:, 4 * H : 4 * (H + OS)].bitcast(I32))
        for i, (g0, n, c0, w) in enumerate(W1_LOADS):
            nc.sync.dma_start(
                out=w1[i][:].bitcast(I32),
                in_=w1_words[g0 : g0 + n].rearrange("g p n t -> p g (n t)")[
                    :, :, 4 * NT * c0 : 4 * NT * (c0 + w)
                ].bitcast(I32),
            )

        xg = keep.tile([P, GX * B * 4], BF16, name="xg", align_bytes=64)
        xq = keep.tile([P, GX * B], U32, name="xq", align_bytes=64)
        xs = keep.tile([P, GX * B], U8, name="xs", align_bytes=64)
        x32 = x_sb[:].bitcast(F32)
        xg32 = xg[:].bitcast(F32).rearrange("p (g b u) -> p g b u", g=GX, u=2)
        for hf in range(2):
            xt = psum.tile([P, 2, 2, B], F32, name="xt_%d" % hf, tag="b%d" % hf)
            for gl in range(2):
                g = 2 * hf + gl
                for u in range(2):
                    nc.tensor.transpose(xt[:, gl, u, :], x32[:, 256 * g + u : 256 * (g + 1) : 2], ident_f[:])
            src = xt[:].rearrange("p g u b -> p g b u")
            if hf == 0:
                nc.vector.tensor_copy(out=xg32[:, 0:2], in_=src)
            else:
                nc.scalar.copy(out=xg32[:, 2:4], in_=src)
        nc.vector.quantize_mx(out=xq[:].bitcast(FP8X4), scales=xs[:], in_=xg[:])

        bias_h = [keep.tile([P, 4, P], BF16, name="bias_h_%d" % j) for j in range(GH)]
        bias_o = [keep.tile([P, NT], BF16, name="bias_o_%d" % c) for c in range(CO)]
        for i in range(GH + CO):
            pb = psum.tile([P, NT], F32, name="pb_%d" % i, tag="b%d" % (2 + i % 6))
            for s in range(4):
                c = 4 * i + s
                nc.tensor.matmul(
                    out=pb[:, P * s : P * (s + 1)],
                    lhsT=ident_b[:, c : c + 1].to_broadcast([P, P]),
                    rhs=bt[:],
                    start=True,
                    stop=True,
                )
            if i < GH:
                dst = bias_h[i][:]
                src = pb[:].rearrange("b (p t) -> b t p", t=4)
            else:
                dst = bias_o[i - GH][:]
                src = pb[:]
            if i % 2 == 0:
                nc.vector.tensor_copy(out=dst, in_=src)
            else:
                nc.scalar.copy(out=dst, in_=src)

        def x_pass(acc, g, words, col0, start, stop):
            nc.tensor.matmul_mx(
                out=acc,
                lhsT=xq[:, B * g : B * (g + 1)].bitcast(FP8X4),
                lhsT_scale=xs[:, B * g : B * (g + 1)],
                rhs=words.bitcast(FP8X4),
                rhs_scale=pl0[4 * g : P, col0 : col0 + NT],
                start=start,
                stop=stop,
            )

        ph = [psum.tile([P, NT], F32, name="ph_%d" % j, tag="b%d" % j) for j in range(GH)]
        for g in range(GX):
            for j in range(GH):
                words = w0[g] if g < GX - 1 else w0h
                x_pass(ph[j][:], g, words[:, NT * j : NT * (j + 1)], NT * j, g == 0, g == GX - 1)

        zb = [keep.tile([P, 4, P], BF16, name="zb_%d" % j) for j in range(GH)]
        hg = [keep.tile([P, 2, B, 4], BF16, name="hg_%d" % jj, align_bytes=64) for jj in range(GH // 2)]
        hq = [keep.tile([P, 2 * B], U32, name="hq_%d" % jj, align_bytes=64) for jj in range(GH // 2)]
        hs = [keep.tile([P, 2 * B], U8, name="hs_%d" % jj, align_bytes=64) for jj in range(GH // 2)]
        for jj in range(GH // 2):
            for jl in range(2):
                j = 2 * jj + jl
                nc.vector.tensor_tensor(
                    out=zb[j][:],
                    in0=ph[j][:].rearrange("b (p t) -> b t p", t=4),
                    in1=bias_h[j][:],
                    op=ADD,
                )
            tp = psum.tile([P, 2, 4, B], BF16, name="tp_%d" % jj, tag="b%d" % jj)
            for jl in range(2):
                for t in range(4):
                    nc.tensor.transpose(tp[:, jl, t, :], zb[2 * jj + jl][:, t, :], ident_b[:])
            nc.scalar.activation(out=hg[jj][:], in_=tp[:].rearrange("p j t b -> p j b t"), func=RELU)
        for jj in range(GH // 2):
            nc.vector.quantize_mx(
                out=hq[jj][:].bitcast(FP8X4),
                scales=hs[jj][:],
                in_=hg[jj][:].rearrange("p j b t -> p (j b t)"),
            )

        po = [psum.tile([P, NT], F32, name="po_%d" % c, tag="b%d" % (4 + c)) for c in range(CO)]
        for g in range(GX):
            for c in range(CO):
                words = w0[g][:, H:] if g < GX - 1 else w0o
                x_pass(po[c][:], g, words[:, NT * c : NT * (c + 1)], H + NT * c, g == 0, False)

        def h_pass(c, g, words):
            nc.tensor.matmul_mx(
                out=po[c][:],
                lhsT=hq[g // 2][:, B * (g % 2) : B * (g % 2 + 1)].bitcast(FP8X4),
                lhsT_scale=hs[g // 2][:, B * (g % 2) : B * (g % 2 + 1)],
                rhs=words.bitcast(FP8X4),
                rhs_scale=pl1[g // 4][4 * (g % 4) : P, NT * c : NT * (c + 1)],
                start=False,
                stop=(g == GH - 1),
            )

        for i, (g0, n, c0, w) in enumerate(W1_LOADS):
            for gl in range(n):
                for c in range(w):
                    h_pass(c0 + c, g0 + gl, w1[i][:, gl, NT * c : NT * (c + 1)])
            if g0 + n < GH:
                continue
            wo = NT if c0 + w < CO else NT // 2
            for lo in range(NT * c0, NT * (c0 + w), wo):
                c, off = divmod(lo, NT)
                o_sb = keep.tile([P, wo], F32, name="o_sb_%d" % lo)
                nc.vector.tensor_tensor(
                    out=o_sb[:], in0=po[c][:, off : off + wo], in1=bias_o[c][:, off : off + wo], op=ADD
                )
                nc.sync.dma_start(out=out[:, lo : lo + wo], in_=o_sb[:])
